import numpy as np
import ml_dtypes


def mxq(x, axis, fmt="e4m3"):
    dtype, down = {"e4m3": (ml_dtypes.float8_e4m3fn, 7), "e5m2": (ml_dtypes.float8_e5m2, 14)}[fmt]
    v = np.moveaxis(np.asarray(x, np.float32).astype(ml_dtypes.bfloat16).astype(np.float64), axis, -1)
    blocks = v.reshape(v.shape[:-1] + (-1, 32))
    amax = np.abs(blocks).max(-1, keepdims=True)
    byte = np.maximum(np.where(amax > 0, np.frexp(amax)[1] - 1 + 127, 0) - down, 1)
    scale = np.exp2(byte - 127.0)
    codes = (blocks / scale).astype(np.float32).astype(dtype).astype(np.float64)
    return np.moveaxis((codes * scale).reshape(v.shape), -1, axis)


WIDE = False


def mx_kscale(k):
    if not WIDE:
        return np.ones(k)
    levels = np.array([10, -10, 5, -5, 0])
    a = np.random.permutation(np.resize(levels, k // 512 * 4)).reshape(k // 512, 4)
    idx = np.arange(k)
    return np.exp2(a[idx // 512, idx % 128 // 32])


BF16 = ml_dtypes.bfloat16


def bf(x):
    return np.asarray(x, np.float32).astype(BF16)


def f64(x):
    return np.asarray(x).astype(np.float64)


E2M1 = np.array([0.0, 0.5, 1.0, 1.5, 2.0, 3.0, 4.0, 6.0, -0.0, -0.5, -1.0, -1.5, -2.0, -3.0, -4.0, -6.0])


def pack_weight(w, fmt):
    k, n = w.shape
    w = f64(bf(w)).reshape(k // 32, 32, n)
    amax = np.abs(w).max(1)
    if fmt == "e4m3":
        byte = np.frexp(amax)[1] - 1 + 127 - 7
    else:
        mant, ex = np.frexp(amax / 6.0)
        byte = np.where(mant > 0.5, ex, ex - 1) + 127
    byte = np.clip(np.where(amax > 0, byte, 1), 1, 254)
    scaled = (w * np.exp2(127.0 - byte)[:, None, :]).reshape(k, n).astype(np.float32)
    by_word = np.ascontiguousarray(scaled.reshape(k // 512, 128, 4, n).transpose(0, 1, 3, 2))
    if fmt == "e4m3":
        words = by_word.astype(ml_dtypes.float8_e4m3fn).view(np.uint8)
    else:
        c = by_word.astype(ml_dtypes.float4_e2m1fn).view(np.uint8) & 0xF
        words = c[..., 0::2] | (c[..., 1::2] << 4)
    return np.ascontiguousarray(words), np.ascontiguousarray(byte.astype(np.uint8).reshape(k // 512, 16, n))


def unpack_weight(words, scales, fmt):
    g, p, n, _ = words.shape
    if fmt == "e4m3":
        vals = np.ascontiguousarray(words).view(ml_dtypes.float8_e4m3fn).astype(np.float64)
    else:
        nib = np.empty((g, p, n, 4), np.uint8)
        nib[..., 0::2] = words & 0xF
        nib[..., 1::2] = words >> 4
        vals = E2M1[nib]
    vals = vals * np.repeat(np.exp2(scales.astype(np.float64) - 127.0), 8, axis=1)[..., None]
    return vals.transpose(0, 1, 3, 2).reshape(g * 512, n)


B, D, S = 512, 512, 1024
EPS = 1e-5
FMT = "e4m3"


def layernorm(v, g, b):
    mu = v.mean(-1, keepdims=True)
    var = ((v - mu) ** 2).mean(-1, keepdims=True)
    return (v - mu) / np.sqrt(var + EPS) * g + b


def sigmoid(v):
    return 1.0 / (1.0 + np.exp(-v))


def setup_inputs():
    a = mx_kscale(D)
    x = bf(np.random.standard_normal((B, D)) * a)
    s_prev0 = bf(np.random.standard_normal((B, S)))
    s_prev1 = bf(np.random.standard_normal((B, S)))
    Wi = np.random.standard_normal((4 * S, D)) / np.sqrt(D) / a[None, :]
    Wi_words, Wi_scales = pack_weight(np.ascontiguousarray(Wi.T), FMT)
    Ws = np.random.standard_normal((4 * S, 2 * S)) / np.sqrt(2 * S)
    Ws_words, Ws_scales = pack_weight(np.ascontiguousarray(Ws.T), FMT)
    return {"x": x,
            "s_prev0": s_prev0,
            "s_prev1": s_prev1,
            "Wi_words": Wi_words,
            "Wi_scales": Wi_scales,
            "Ws_words": Ws_words,
            "Ws_scales": Ws_scales,
            "lni_g": bf(1.0 + 0.1 * np.random.standard_normal(4 * S)),
            "lni_b": bf(0.1 * np.random.standard_normal(4 * S)),
            "lns_g": bf(1.0 + 0.1 * np.random.standard_normal(4 * S)),
            "lns_b": bf(0.1 * np.random.standard_normal(4 * S)),
            "lnh_g": bf(1.0 + 0.1 * np.random.standard_normal(S)),
            "lnh_b": bf(0.1 * np.random.standard_normal(S))}


def reference(x, s_prev0, s_prev1, Wi_words, Wi_scales, Ws_words, Ws_scales, lni_g, lni_b, lns_g, lns_b, lnh_g, lnh_b):
    p0, p1 = f64(s_prev0), f64(s_prev1)
    s = np.concatenate([p0, p1], axis=-1)
    igates = layernorm(mxq(f64(x), 1, "e4m3") @ unpack_weight(Wi_words, Wi_scales, FMT), f64(lni_g), f64(lni_b))
    sgates = layernorm(mxq(s, 1, "e4m3") @ unpack_weight(Ws_words, Ws_scales, FMT), f64(lns_g), f64(lns_b))
    gates = igates + sgates
    r_inv, i, n, l = np.split(gates, 4, axis=1)
    s_n = sgates[:, 2 * S:3 * S]
    l = sigmoid(l)
    r_inv = sigmoid(r_inv)
    i = sigmoid(i)
    n = np.tanh(n - r_inv * s_n)
    h = n + i * (l * p0 + (1.0 - l) * p1 - n)
    return layernorm(h, f64(lnh_g), f64(lnh_b))

@@ -1,0 +1,320 @@
+from contextlib import ExitStack
+
+import concourse.mybir as mybir
+from concourse.masks import make_identity
+
+BF16 = mybir.dt.bfloat16
+F32 = mybir.dt.float32
+I32 = mybir.dt.int32
+U32 = mybir.dt.uint32
+U8 = mybir.dt.uint8
+FP8X4 = mybir.dt.float8_e4m3fn_x4
+ALU = mybir.AluOpType
+ACT = mybir.ActivationFunctionType
+
+P = 128
+PACK = 4
+K_PASS = P * PACK
+BATCH, D_IN, STATE = 512, 512, 1024
+GATES = 4 * STATE
+EPS = 1e-5
+BATCH_TILES = BATCH // P
+BANK = 512
+BANKS_PER_ROW = GATES // BANK
+STATE_PASSES = 2 * STATE // K_PASS
+WORDS = K_PASS // 2
+ROUND = 4
+
+RESET = slice(0 * STATE, 1 * STATE)
+INPUT = slice(1 * STATE, 2 * STATE)
+CAND_FIRST = 2 * STATE
+CAND = slice(CAND_FIRST, CAND_FIRST + STATE)
+LERP = slice(3 * STATE, 4 * STATE)
+
+ROW_LNS_G, ROW_LNI_B, ROW_LNS_B = 0, 32, 64
+
+FLOPS = 2 * BATCH * GATES * (D_IN + 2 * STATE)
+
+
+def tile_lngru2dcell_kernel(
+    tc, x, s_prev0, s_prev1, Wi_words, Wi_scales, Ws_words, Ws_scales,
+    lni_g, lni_b, lns_g, lns_b, lnh_g, lnh_b, out,
+):
+    nc = tc.nc
+    with ExitStack() as ctx:
+        keep = ctx.enter_context(tc.tile_pool(name="keep", bufs=1))
+        stage = ctx.enter_context(tc.tile_pool(name="stage", bufs=2))
+        gates = ctx.enter_context(tc.tile_pool(name="gates", bufs=2))
+        blend = ctx.enter_context(tc.tile_pool(name="blend", bufs=2))
+        stat = ctx.enter_context(tc.tile_pool(name="stat", bufs=4))
+        psum_gain = ctx.enter_context(tc.psum_pool(name="psum_gain", bufs=1))
+        psum_acc = ctx.enter_context(tc.psum_pool(name="psum_acc", bufs=2))
+        psum_bias = ctx.enter_context(tc.psum_pool(name="psum_bias", bufs=2))
+
+        x_sb = keep.tile([P, BATCH_TILES, D_IN], BF16)
+        p0_sb = keep.tile([P, BATCH_TILES, STATE], BF16)
+        p1_sb = keep.tile([P, BATCH_TILES, STATE], BF16)
+        wi_words = keep.tile([P, GATES], U32, align_bytes=64)
+        ws_words = keep.tile([P, STATE_PASSES, GATES], U32, align_bytes=64)
+        wi_plane = keep.tile([P, GATES], U8, align_bytes=64)
+        ws_planes = keep.tile([P, GATES], U8, align_bytes=64)
+        n_operands = BATCH_TILES * (1 + STATE_PASSES)
+        act_codes = keep.tile([P, n_operands, P], U32, align_bytes=64)
+        act_scales = keep.tile([P, n_operands, P], U8, align_bytes=64)
+        rows = keep.tile([P, GATES], BF16)
+        lni_g_all = keep.tile([P, GATES], BF16)
+        lnh_g_all = keep.tile([P, STATE], BF16)
+        lnh_b_all = keep.tile([P, STATE], BF16)
+        ident = keep.tile([P, P], F32)
+        pick = keep.tile([P, 4, P], BF16)
+        neg_half = keep.tile([P, 1], F32)
+        zero_col = keep.tile([P, 1], F32)
+        warm_col = keep.tile([P, 1], F32)
+        squares = keep.tile([P, STATE], F32)
+
+        nc.vector.memset(wi_plane[:].bitcast(I32), 0)
+        nc.vector.memset(ws_planes[:].bitcast(I32), 0)
+        nc.vector.memset(zero_col[:], 0.0)
+        nc.vector.memset(neg_half[:], -0.5)
+        nc.vector.memset(rows[:].bitcast(I32), 0)
+        nc.vector.memset(pick[:], 0.0)
+        PICK_LNS_G, PICK_BOTH_B, PICK_LNI_B, PICK_LNS_B = 0, 1, 2, 3
+        nc.vector.memset(pick[ROW_LNS_G : ROW_LNS_G + 1, PICK_LNS_G, :], 1.0)
+        nc.vector.memset(pick[ROW_LNI_B : ROW_LNI_B + 1, PICK_BOTH_B, :], 1.0)
+        nc.vector.memset(pick[ROW_LNS_B : ROW_LNS_B + 1, PICK_BOTH_B, :], 1.0)
+        nc.vector.memset(pick[ROW_LNI_B : ROW_LNI_B + 1, PICK_LNI_B, :], 1.0)
+        nc.vector.memset(pick[ROW_LNS_B : ROW_LNS_B + 1, PICK_LNS_B, :], 1.0)
+        make_identity(nc, ident[:])
+        nc.scalar.activation(out=warm_col[:], in_=zero_col[:], func=ACT.Sigmoid)
+
+        nc.sync.dma_start(out=x_sb[:], in_=x.rearrange("(m p) d -> p m d", p=P))
+        for quad in range(4):
+            nc.sync.dma_start(
+                out=wi_plane[32 * quad : 32 * quad + 4, :].bitcast(I32),
+                in_=Wi_scales[0, 4 * quad : 4 * quad + 4, :].bitcast(I32),
+            )
+        wi_dram = Wi_words[0].rearrange("p n t -> p (n t)").bitcast(I32)
+        for c in range(4):
+            cols = slice(c * STATE, (c + 1) * STATE)
+            nc.sync.dma_start(out=wi_words[:, cols].bitcast(I32), in_=wi_dram[:, cols])
+        for quad in range(4):
+            nc.sync.dma_start(
+                out=ws_planes[32 * quad : 32 * quad + 16, :].bitcast(I32),
+                in_=Ws_scales[:, 4 * quad : 4 * quad + 4, :].bitcast(I32),
+            )
+        ws_dram = Ws_words.rearrange("g p n t -> p g (n t)").bitcast(I32)
+        for n in range(BANKS_PER_ROW):
+            cols = slice(n * BANK, (n + 1) * BANK)
+            nc.sync.dma_start(out=ws_words[:, :, cols].bitcast(I32), in_=ws_dram[:, :, cols])
+        nc.scalar.dma_start(out=rows[ROW_LNS_G : ROW_LNS_G + 1, :], in_=lns_g.unsqueeze(0))
+        nc.scalar.dma_start(out=rows[ROW_LNI_B : ROW_LNI_B + 1, :], in_=lni_b.unsqueeze(0))
+        nc.scalar.dma_start(out=rows[ROW_LNS_B : ROW_LNS_B + 1, :], in_=lns_b.unsqueeze(0))
+        nc.scalar.dma_start(out=lni_g_all[:], in_=lni_g.partition_broadcast(P))
+        nc.scalar.dma_start(out=p0_sb[:], in_=s_prev0.rearrange("(m p) d -> p m d", p=P))
+        nc.scalar.dma_start(out=p1_sb[:], in_=s_prev1.rearrange("(m p) d -> p m d", p=P))
+        nc.scalar.dma_start(out=lnh_g_all[:], in_=lnh_g.partition_broadcast(P))
+        nc.scalar.dma_start(out=lnh_b_all[:], in_=lnh_b.partition_broadcast(P))
+
+        def quantise_round(first_operand, sources):
+            grouped = stage.tile([P, ROUND, P, PACK], BF16, align_bytes=64)
+            grouped_words = grouped[:].rearrange("p c b t -> p (c b t)").bitcast(F32)
+            for half in range(2):
+                flipped = psum_acc.tile([P, 4, P], F32, tag="acc")
+                for c in range(2):
+                    for u in range(2):
+                        nc.tensor.transpose(
+                            flipped[:, 2 * c + u, :], sources[2 * half + c][:, u:WORDS:2], ident[:]
+                        )
+                dst = grouped_words[:, half * BANK : (half + 1) * BANK]
+                dst = dst.rearrange("p (c b u) -> p c b u", c=2, u=2)
+                src = flipped[:].rearrange("p (c u) b -> p c b u", u=2)
+                if half == 0:
+                    nc.vector.tensor_copy(out=dst, in_=src)
+                else:
+                    nc.scalar.copy(out=dst, in_=src)
+            taken = slice(first_operand, first_operand + ROUND)
+            nc.vector.quantize_mx(
+                out=act_codes[:, taken, :].rearrange("p c b -> p (c b)").bitcast(FP8X4),
+                scales=act_scales[:, taken, :].rearrange("p c b -> p (c b)"),
+                in_=grouped[:].rearrange("p c b t -> p (c b t)"),
+            )
+
+        quantise_round(0, [x_sb[:, m, :].bitcast(F32) for m in range(BATCH_TILES)])
+
+        lns_g_banks = []
+        for c in range(4):
+            gain = psum_gain.tile([P, STATE], BF16, name="lns_g_bank%d" % c)
+            for h in range(2):
+                nc.tensor.matmul(
+                    out=gain[:, h * BANK : (h + 1) * BANK],
+                    lhsT=pick[:, PICK_LNS_G, :],
+                    rhs=rows[:, c * STATE + h * BANK : c * STATE + (h + 1) * BANK],
+                    start=True,
+                    stop=True,
+                )
+            lns_g_banks.append(gain)
+
+        def quantise_states():
+            for m in range(BATCH_TILES):
+                p0_words = p0_sb[:, m, :].bitcast(F32)
+                p1_words = p1_sb[:, m, :].bitcast(F32)
+                quantise_round(
+                    BATCH_TILES + STATE_PASSES * m,
+                    [p0_words[:, 0:WORDS], p0_words[:, WORDS : 2 * WORDS],
+                     p1_words[:, 0:WORDS], p1_words[:, WORDS : 2 * WORDS]],
+                )
+
+        def row_total(parts, width, factor):
+            scaled = stat.tile([P, BANKS_PER_ROW], F32)
+            total = stat.tile([P, 1], F32)
+            nc.scalar.activation(
+                out=scaled[:, 0:width], in_=parts[:], func=ACT.Copy, scale=factor, accum_out=total[:]
+            )
+            return total
+
+        def rsqrt(variance):
+            shifted = stat.tile([P, 1], F32)
+            nc.gpsimd.tensor_scalar(
+                out=shifted[:], in0=variance, scalar1=1.0, scalar2=EPS, op0=ALU.mult, op1=ALU.add
+            )
+            rstd = stat.tile([P, 1], F32)
+            nc.gpsimd.tensor_tensor(out=rstd[:], in0=shifted[:], in1=neg_half[:], op=ALU.pow)
+            return rstd
+
+        def product(raw, passes):
+            bank_sums = stat.tile([P, BANKS_PER_ROW], F32)
+            for n in range(BANKS_PER_ROW):
+                cols = slice(n * BANK, (n + 1) * BANK)
+                acc = psum_acc.tile([P, BANK], F32, tag="acc")
+                for j, (operand, words, plane) in enumerate(passes):
+                    nc.tensor.matmul_mx(
+                        out=acc[:],
+                        lhsT=act_codes[:, operand, :].bitcast(FP8X4),
+                        lhsT_scale=act_scales[:, operand, :],
+                        rhs=words[:, cols].bitcast(FP8X4),
+                        rhs_scale=plane[:, cols],
+                        start=(j == 0),
+                        stop=(j == len(passes) - 1),
+                    )
+                nc.scalar.activation(
+                    out=raw[:, cols], in_=acc[:], func=ACT.Copy, accum_out=bank_sums[:, n : n + 1]
+                )
+            return row_total(bank_sums, BANKS_PER_ROW, -1.0 / GATES)
+
+        def centre_and_gain(raw, neg_mean, gain_of_block):
+            block_squares = stat.tile([P, 4], F32)
+            for c in range(4):
+                cols = slice(c * STATE, (c + 1) * STATE)
+                nc.scalar.activation(
+                    out=squares[:], in_=raw[:, cols], func=ACT.Square, bias=neg_mean[:, 0:1], scale=1.0,
+                    accum_out=block_squares[:, c : c + 1],
+                )
+                nc.vector.scalar_tensor_tensor(
+                    out=raw[:, cols], in0=raw[:, cols], scalar=neg_mean[:, 0:1], in1=gain_of_block(c),
+                    op0=ALU.add, op1=ALU.mult,
+                )
+            return rsqrt(row_total(block_squares, 4, 1.0 / GATES)[:])
+
+        def scale_and_bias(tile_, cols, rstd, picked):
+            bias = psum_bias.tile([P, BANK], F32, tag="bias")
+            nc.tensor.matmul(out=bias[:], lhsT=pick[:, picked, :], rhs=rows[:, cols], start=True, stop=True)
+            nc.vector.scalar_tensor_tensor(
+                out=tile_[:, cols], in0=tile_[:, cols], scalar=rstd[:, 0:1], in1=bias[:],
+                op0=ALU.mult, op1=ALU.add,
+            )
+
+        def input_product(m):
+            ig = gates.tile([P, GATES], F32, tag="ig")
+            return ig, product(ig, [(m, wi_words, wi_plane)])
+
+        def input_centre(ig, neg_mean):
+            return centre_and_gain(ig, neg_mean, lambda c: lni_g_all[:, c * STATE : (c + 1) * STATE])
+
+        def input_bias(ig, rstd):
+            for n in range(BANKS_PER_ROW):
+                in_cand = CAND_FIRST <= n * BANK < CAND_FIRST + STATE
+                scale_and_bias(ig, slice(n * BANK, (n + 1) * BANK), rstd, PICK_LNI_B if in_cand else PICK_BOTH_B)
+
+        def state_product(m):
+            sg = gates.tile([P, GATES], F32, tag="sg")
+            first = BATCH_TILES + STATE_PASSES * m
+            neg_mean = product(
+                sg,
+                [(first + g, ws_words[:, g, :], ws_planes[4 * g : P, :]) for g in range(STATE_PASSES)],
+            )
+            return sg, neg_mean
+
+        def state_centre(sg, neg_mean):
+            return centre_and_gain(sg, neg_mean, lambda c: lns_g_banks[c][:])
+
+        def finish(m, ig, sg, rstd, helper):
+            p0 = p0_sb[:, m, :]
+            p1 = p1_sb[:, m, :]
+
+            def add_gates(block):
+                nc.vector.scalar_tensor_tensor(
+                    out=sg[:, block], in0=sg[:, block], scalar=rstd[:, 0:1], in1=ig[:, block],
+                    op0=ALU.mult, op1=ALU.add,
+                )
+
+            mix = blend.tile([P, STATE], F32)
+            nc.gpsimd.tensor_tensor(out=mix[:], in0=p0, in1=p1, op=ALU.subtract)
+
+            add_gates(RESET)
+            nc.scalar.activation(out=sg[:, RESET], in_=sg[:, RESET], func=ACT.Sigmoid, scale=-1.0)
+            for h in range(2):
+                scale_and_bias(sg, slice(CAND_FIRST + h * BANK, CAND_FIRST + (h + 1) * BANK), rstd, PICK_LNS_B)
+            add_gates(LERP)
+            nc.scalar.activation(out=sg[:, LERP], in_=sg[:, LERP], func=ACT.Sigmoid)
+            add_gates(INPUT)
+            nc.scalar.activation(out=sg[:, INPUT], in_=sg[:, INPUT], func=ACT.Sigmoid)
+            helper.tensor_tensor(out=sg[:, CAND], in0=sg[:, CAND], in1=sg[:, RESET], op=ALU.mult)
+            helper.tensor_tensor(out=sg[:, CAND], in0=sg[:, CAND], in1=ig[:, CAND], op=ALU.add)
+            nc.scalar.activation(out=sg[:, CAND], in_=sg[:, CAND], func=ACT.Tanh)
+
+            nc.gpsimd.tensor_tensor(out=mix[:], in0=mix[:], in1=sg[:, LERP], op=ALU.mult)
+            nc.gpsimd.tensor_tensor(out=mix[:], in0=mix[:], in1=p1, op=ALU.add)
+            helper.tensor_tensor(out=mix[:], in0=mix[:], in1=sg[:, CAND], op=ALU.subtract)
+            helper.tensor_tensor(out=mix[:], in0=mix[:], in1=sg[:, INPUT], op=ALU.mult)
+            helper.tensor_tensor(out=mix[:], in0=mix[:], in1=sg[:, CAND], op=ALU.add)
+
+            chunk_stats = stat.tile([P, 2, 6], F32)
+            for h in range(2):
+                nc.vector.bn_stats(out=chunk_stats[:, h, :], in_=mix[:, h * BANK : (h + 1) * BANK])
+            mean_var = stat.tile([P, 2], F32)
+            nc.vector.bn_aggr(out=mean_var[:], in_=chunk_stats[:].rearrange("p a b -> p (a b)"))
+            rstd_h = rsqrt(mean_var[:, 1:2])
+            nc.vector.scalar_tensor_tensor(
+                out=mix[:], in0=mix[:], scalar=mean_var[:, 0:1], in1=lnh_g_all[:],
+                op0=ALU.subtract, op1=ALU.mult,
+            )
+            nc.vector.scalar_tensor_tensor(
+                out=mix[:], in0=mix[:], scalar=rstd_h[:, 0:1], in1=lnh_b_all[:],
+                op0=ALU.mult, op1=ALU.add,
+            )
+            nc.sync.dma_start(out=out[m * P : (m + 1) * P, :], in_=mix[:])
+
+        ig_of = {}
+        sg_of = {}
+
+        def input_gates_first_half(m):
+            ig, neg_mean = input_product(m)
+            ig_of[m] = (ig, input_centre(ig, neg_mean))
+
+        input_gates_first_half(0)
+        quantise_states()
+        input_gates_first_half(1)
+        input_bias(*ig_of[0])
+        sg_of[0] = state_product(0)
+        input_bias(*ig_of[1])
+        rstd_of = {0: state_centre(*sg_of[0])}
+        for m in range(BATCH_TILES):
+            if m + 1 < BATCH_TILES:
+                sg_of[m + 1] = state_product(m + 1)
+            finish(m, ig_of[m][0], sg_of[m][0], rstd_of[m], nc.vector if m == BATCH_TILES - 1 else nc.gpsimd)
+            if m + 2 < BATCH_TILES:
+                input_gates_first_half(m + 2)
+            if m + 1 < BATCH_TILES:
+                rstd_of[m + 1] = state_centre(*sg_of[m + 1])
+            if m + 2 < BATCH_TILES:
+                input_bias(*ig_of[m + 2])

@@ -44,12 +44,12 @@ def tile_lngru2dcell_kernel(
     with ExitStack() as ctx:
         keep = ctx.enter_context(tc.tile_pool(name="keep", bufs=1))
         stage = ctx.enter_context(tc.tile_pool(name="stage", bufs=2))
-        gates = ctx.enter_context(tc.tile_pool(name="gates", bufs=2))
         blend = ctx.enter_context(tc.tile_pool(name="blend", bufs=2))
         stat = ctx.enter_context(tc.tile_pool(name="stat", bufs=4))
         psum_gain = ctx.enter_context(tc.psum_pool(name="psum_gain", bufs=1))
         psum_acc = ctx.enter_context(tc.psum_pool(name="psum_acc", bufs=2))
         psum_bias = ctx.enter_context(tc.psum_pool(name="psum_bias", bufs=2))
+        ctx.enter_context(tc.manual_schedule())
 
         x_sb = keep.tile([P, BATCH_TILES, D_IN], BF16)
         p0_sb = keep.tile([P, BATCH_TILES, STATE], BF16)
@@ -70,7 +70,9 @@ def tile_lngru2dcell_kernel(
         neg_half = keep.tile([P, 1], F32)
         zero_col = keep.tile([P, 1], F32)
         warm_col = keep.tile([P, 1], F32)
-        squares = keep.tile([P, STATE], F32)
+        squares = keep.tile([P, BANK], F32)
+        ig_tiles = [keep.tile([P, GATES], F32, name="ig%d" % i) for i in range(2)]
+        sg_tiles = [keep.tile([P, GATES], F32, name="sg%d" % i) for i in range(2)]
 
         nc.vector.memset(wi_plane[:].bitcast(I32), 0)
         nc.vector.memset(ws_planes[:].bitcast(I32), 0)
@@ -154,22 +156,22 @@ def tile_lngru2dcell_kernel(
                 )
             lns_g_banks.append(gain)
 
-        def quantise_states():
-            for m in range(BATCH_TILES):
-                p0_words = p0_sb[:, m, :].bitcast(F32)
-                p1_words = p1_sb[:, m, :].bitcast(F32)
-                quantise_round(
-                    BATCH_TILES + STATE_PASSES * m,
-                    [p0_words[:, 0:WORDS], p0_words[:, WORDS : 2 * WORDS],
-                     p1_words[:, 0:WORDS], p1_words[:, WORDS : 2 * WORDS]],
-                )
+        def quantise_states(m):
+            p0_words = p0_sb[:, m, :].bitcast(F32)
+            p1_words = p1_sb[:, m, :].bitcast(F32)
+            quantise_round(
+                BATCH_TILES + STATE_PASSES * m,
+                [p0_words[:, 0:WORDS], p0_words[:, WORDS : 2 * WORDS],
+                 p1_words[:, 0:WORDS], p1_words[:, WORDS : 2 * WORDS]],
+            )
 
-        def row_total(parts, width, factor):
+        def bank_cols(n):
+            return slice(n * BANK, (n + 1) * BANK)
+
+        def row_total(parts, factor):
             scaled = stat.tile([P, BANKS_PER_ROW], F32)
             total = stat.tile([P, 1], F32)
-            nc.scalar.activation(
-                out=scaled[:, 0:width], in_=parts[:], func=ACT.Copy, scale=factor, accum_out=total[:]
-            )
+            nc.scalar.activation(out=scaled[:], in_=parts[:], func=ACT.Copy, scale=factor, accum_out=total[:])
             return total
 
         def rsqrt(variance):
@@ -181,140 +183,154 @@ def tile_lngru2dcell_kernel(
             nc.gpsimd.tensor_tensor(out=rstd[:], in0=shifted[:], in1=neg_half[:], op=ALU.pow)
             return rstd
 
-        def product(raw, passes):
-            bank_sums = stat.tile([P, BANKS_PER_ROW], F32)
-            for n in range(BANKS_PER_ROW):
-                cols = slice(n * BANK, (n + 1) * BANK)
-                acc = psum_acc.tile([P, BANK], F32, tag="acc")
-                for j, (operand, words, plane) in enumerate(passes):
-                    nc.tensor.matmul_mx(
-                        out=acc[:],
-                        lhsT=act_codes[:, operand, :].bitcast(FP8X4),
-                        lhsT_scale=act_scales[:, operand, :],
-                        rhs=words[:, cols].bitcast(FP8X4),
-                        rhs_scale=plane[:, cols],
-                        start=(j == 0),
-                        stop=(j == len(passes) - 1),
-                    )
-                nc.scalar.activation(
-                    out=raw[:, cols], in_=acc[:], func=ACT.Copy, accum_out=bank_sums[:, n : n + 1]
-                )
-            return row_total(bank_sums, BANKS_PER_ROW, -1.0 / GATES)
+        n_matrices = 2 * BATCH_TILES
+        sums_of = {}
+        norm_of = {}
 
-        def centre_and_gain(raw, neg_mean, gain_of_block):
-            block_squares = stat.tile([P, 4], F32)
-            for c in range(4):
-                cols = slice(c * STATE, (c + 1) * STATE)
-                nc.scalar.activation(
-                    out=squares[:], in_=raw[:, cols], func=ACT.Square, bias=neg_mean[:, 0:1], scale=1.0,
-                    accum_out=block_squares[:, c : c + 1],
-                )
-                nc.vector.scalar_tensor_tensor(
-                    out=raw[:, cols], in0=raw[:, cols], scalar=neg_mean[:, 0:1], in1=gain_of_block(c),
-                    op0=ALU.add, op1=ALU.mult,
-                )
-            return rsqrt(row_total(block_squares, 4, 1.0 / GATES)[:])
+        def raw_tile(matrix):
+            return (sg_tiles if matrix % 2 else ig_tiles)[(matrix // 2) % 2]
 
-        def scale_and_bias(tile_, cols, rstd, picked):
+        def sweep_step(matrix, n):
+            m = matrix // 2
+            if matrix % 2:
+                first = BATCH_TILES + STATE_PASSES * m
+                passes = [(first + g, ws_words[:, g, :], ws_planes[4 * g : P, :]) for g in range(STATE_PASSES)]
+            else:
+                passes = [(m, wi_words, wi_plane)]
+            raw = raw_tile(matrix)
+            cols = bank_cols(n)
+            if n == 0:
+                bank_sums = stat.tile([P, BANKS_PER_ROW], F32)
+                bank_squares = stat.tile([P, BANKS_PER_ROW], F32)
+                neg_shift = stat.tile([P, 1], F32)
+                sums_of[matrix] = (bank_sums, bank_squares, neg_shift)
+            bank_sums, bank_squares, neg_shift = sums_of[matrix]
+            acc = psum_acc.tile([P, BANK], F32, tag="acc")
+            for j, (operand, words, plane) in enumerate(passes):
+                nc.tensor.matmul_mx(
+                    out=acc[:],
+                    lhsT=act_codes[:, operand, :].bitcast(FP8X4),
+                    lhsT_scale=act_scales[:, operand, :],
+                    rhs=words[:, cols].bitcast(FP8X4),
+                    rhs_scale=plane[:, cols],
+                    start=(j == 0),
+                    stop=(j == len(passes) - 1),
+                )
+            nc.scalar.activation(out=raw[:, cols], in_=acc[:], func=ACT.Copy, accum_out=bank_sums[:, n : n + 1])
+            if n == 0:
+                nc.scalar.mul(out=neg_shift[:], in_=bank_sums[:, 0:1], mul=-1.0 / BANK)
+            nc.scalar.activation(
+                out=squares[:], in_=raw[:, cols], func=ACT.Square, bias=neg_shift[:, 0:1], scale=1.0,
+                accum_out=bank_squares[:, n : n + 1],
+            )
+            if n == BANKS_PER_ROW - 1:
+                neg_mean = row_total(bank_sums, -1.0 / GATES)
+                mean_square = row_total(bank_squares, 1.0 / GATES)
+                offset_square = stat.tile([P, 1], F32)
+                nc.scalar.activation(
+                    out=offset_square[:], in_=neg_mean[:], func=ACT.Square, bias=neg_shift[:, 0:1], scale=-1.0
+                )
+                variance = stat.tile([P, 1], F32)
+                nc.gpsimd.tensor_tensor(out=variance[:], in0=mean_square[:], in1=offset_square[:], op=ALU.subtract)
+                norm_of[matrix] = (neg_mean, rsqrt(variance[:]))
+
+        def centre_and_gain(matrix, block, gain):
+            raw = raw_tile(matrix)
+            nc.vector.scalar_tensor_tensor(
+                out=raw[:, block], in0=raw[:, block], scalar=norm_of[matrix][0][:, 0:1], in1=gain,
+                op0=ALU.add, op1=ALU.mult,
+            )
+
+        def scale_and_bias(matrix, cols, picked):
+            raw = raw_tile(matrix)
             bias = psum_bias.tile([P, BANK], F32, tag="bias")
             nc.tensor.matmul(out=bias[:], lhsT=pick[:, picked, :], rhs=rows[:, cols], start=True, stop=True)
             nc.vector.scalar_tensor_tensor(
-                out=tile_[:, cols], in0=tile_[:, cols], scalar=rstd[:, 0:1], in1=bias[:],
+                out=raw[:, cols], in0=raw[:, cols], scalar=norm_of[matrix][1][:, 0:1], in1=bias[:],
                 op0=ALU.mult, op1=ALU.add,
             )
 
-        def input_product(m):
-            ig = gates.tile([P, GATES], F32, tag="ig")
-            return ig, product(ig, [(m, wi_words, wi_plane)])
+        def input_step(m, n):
+            if n % 2 == 0:
+                block = slice(n * BANK, (n + 2) * BANK)
+                centre_and_gain(2 * m, block, lni_g_all[:, block])
+            in_cand = CAND_FIRST <= n * BANK < CAND_FIRST + STATE
+            scale_and_bias(2 * m, bank_cols(n), PICK_LNI_B if in_cand else PICK_BOTH_B)
 
-        def input_centre(ig, neg_mean):
-            return centre_and_gain(ig, neg_mean, lambda c: lni_g_all[:, c * STATE : (c + 1) * STATE])
+        mix_of = {}
+        last_norm_of = {}
+        block_order = [RESET, CAND, LERP, INPUT]
+        gain_bank_of_block = [0, 2, 3, 1]
 
-        def input_bias(ig, rstd):
-            for n in range(BANKS_PER_ROW):
-                in_cand = CAND_FIRST <= n * BANK < CAND_FIRST + STATE
-                scale_and_bias(ig, slice(n * BANK, (n + 1) * BANK), rstd, PICK_LNI_B if in_cand else PICK_BOTH_B)
-
-        def state_product(m):
-            sg = gates.tile([P, GATES], F32, tag="sg")
-            first = BATCH_TILES + STATE_PASSES * m
-            neg_mean = product(
-                sg,
-                [(first + g, ws_words[:, g, :], ws_planes[4 * g : P, :]) for g in range(STATE_PASSES)],
-            )
-            return sg, neg_mean
-
-        def state_centre(sg, neg_mean):
-            return centre_and_gain(sg, neg_mean, lambda c: lns_g_banks[c][:])
-
-        def finish(m, ig, sg, rstd, helper):
+        def state_step(m, t):
+            ig = ig_tiles[m % 2]
+            sg = sg_tiles[m % 2]
             p0 = p0_sb[:, m, :]
             p1 = p1_sb[:, m, :]
-
-            def add_gates(block):
+            rstd = norm_of[2 * m + 1][1]
+            helper = nc.vector if m == BATCH_TILES - 1 else nc.gpsimd
+            if t == 0:
+                mix_of[m] = blend.tile([P, STATE], F32, name="mix")
+                nc.gpsimd.tensor_tensor(out=mix_of[m][:], in0=p0, in1=p1, op=ALU.subtract)
+            mix = mix_of[m]
+            if t < 8 and t % 2 == 0:
+                centre_and_gain(2 * m + 1, block_order[t // 2], lns_g_banks[gain_bank_of_block[t // 2]][:])
+            if t == 3:
+                for h in range(2):
+                    scale_and_bias(2 * m + 1, bank_cols(CAND_FIRST // BANK + h), PICK_LNS_B)
+            if t in (1, 5, 7):
+                block = block_order[t // 2]
                 nc.vector.scalar_tensor_tensor(
                     out=sg[:, block], in0=sg[:, block], scalar=rstd[:, 0:1], in1=ig[:, block],
                     op0=ALU.mult, op1=ALU.add,
                 )
+            if t == 3:
+                nc.scalar.activation(out=sg[:, RESET], in_=sg[:, RESET], func=ACT.Sigmoid, scale=-1.0)
+            if t == 5:
+                helper.tensor_tensor(out=sg[:, CAND], in0=sg[:, CAND], in1=sg[:, RESET], op=ALU.mult)
+                helper.tensor_tensor(out=sg[:, CAND], in0=sg[:, CAND], in1=ig[:, CAND], op=ALU.add)
+            if t == 7:
+                nc.scalar.activation(out=sg[:, LERP], in_=sg[:, LERP], func=ACT.Sigmoid)
+            if t == 8:
+                nc.gpsimd.tensor_tensor(out=mix[:], in0=mix[:], in1=sg[:, LERP], op=ALU.mult)
+                nc.gpsimd.tensor_tensor(out=mix[:], in0=mix[:], in1=p1, op=ALU.add)
+            if t == 9:
+                nc.scalar.activation(out=sg[:, INPUT], in_=sg[:, INPUT], func=ACT.Sigmoid)
+            if t == 10:
+                nc.scalar.activation(out=sg[:, CAND], in_=sg[:, CAND], func=ACT.Tanh)
+            if t == 11:
+                helper.tensor_tensor(out=mix[:], in0=mix[:], in1=sg[:, CAND], op=ALU.subtract)
+                helper.tensor_tensor(out=mix[:], in0=mix[:], in1=sg[:, INPUT], op=ALU.mult)
+                helper.tensor_tensor(out=mix[:], in0=mix[:], in1=sg[:, CAND], op=ALU.add)
+            if t == 24:
+                chunk_stats = stat.tile([P, 2, 6], F32)
+                for h in range(2):
+                    nc.vector.bn_stats(out=chunk_stats[:, h, :], in_=mix[:, bank_cols(h)])
+                mean_var = stat.tile([P, 2], F32)
+                nc.vector.bn_aggr(out=mean_var[:], in_=chunk_stats[:].rearrange("p a b -> p (a b)"))
+                last_norm_of[m] = (mean_var, rsqrt(mean_var[:, 1:2]))
+            if t == 26:
+                nc.vector.scalar_tensor_tensor(
+                    out=mix[:], in0=mix[:], scalar=last_norm_of[m][0][:, 0:1], in1=lnh_g_all[:],
+                    op0=ALU.subtract, op1=ALU.mult,
+                )
+            if t == 28:
+                nc.vector.scalar_tensor_tensor(
+                    out=mix[:], in0=mix[:], scalar=last_norm_of[m][1][:, 0:1], in1=lnh_b_all[:],
+                    op0=ALU.mult, op1=ALU.add,
+                )
+                nc.sync.dma_start(out=out[m * P : (m + 1) * P, :], in_=mix[:])
 
-            mix = blend.tile([P, STATE], F32)
-            nc.gpsimd.tensor_tensor(out=mix[:], in0=p0, in1=p1, op=ALU.subtract)
-
-            add_gates(RESET)
-            nc.scalar.activation(out=sg[:, RESET], in_=sg[:, RESET], func=ACT.Sigmoid, scale=-1.0)
-            for h in range(2):
-                scale_and_bias(sg, slice(CAND_FIRST + h * BANK, CAND_FIRST + (h + 1) * BANK), rstd, PICK_LNS_B)
-            add_gates(LERP)
-            nc.scalar.activation(out=sg[:, LERP], in_=sg[:, LERP], func=ACT.Sigmoid)
-            add_gates(INPUT)
-            nc.scalar.activation(out=sg[:, INPUT], in_=sg[:, INPUT], func=ACT.Sigmoid)
-            helper.tensor_tensor(out=sg[:, CAND], in0=sg[:, CAND], in1=sg[:, RESET], op=ALU.mult)
-            helper.tensor_tensor(out=sg[:, CAND], in0=sg[:, CAND], in1=ig[:, CAND], op=ALU.add)
-            nc.scalar.activation(out=sg[:, CAND], in_=sg[:, CAND], func=ACT.Tanh)
-
-            nc.gpsimd.tensor_tensor(out=mix[:], in0=mix[:], in1=sg[:, LERP], op=ALU.mult)
-            nc.gpsimd.tensor_tensor(out=mix[:], in0=mix[:], in1=p1, op=ALU.add)
-            helper.tensor_tensor(out=mix[:], in0=mix[:], in1=sg[:, CAND], op=ALU.subtract)
-            helper.tensor_tensor(out=mix[:], in0=mix[:], in1=sg[:, INPUT], op=ALU.mult)
-            helper.tensor_tensor(out=mix[:], in0=mix[:], in1=sg[:, CAND], op=ALU.add)
-
-            chunk_stats = stat.tile([P, 2, 6], F32)
-            for h in range(2):
-                nc.vector.bn_stats(out=chunk_stats[:, h, :], in_=mix[:, h * BANK : (h + 1) * BANK])
-            mean_var = stat.tile([P, 2], F32)
-            nc.vector.bn_aggr(out=mean_var[:], in_=chunk_stats[:].rearrange("p a b -> p (a b)"))
-            rstd_h = rsqrt(mean_var[:, 1:2])
-            nc.vector.scalar_tensor_tensor(
-                out=mix[:], in0=mix[:], scalar=mean_var[:, 0:1], in1=lnh_g_all[:],
-                op0=ALU.subtract, op1=ALU.mult,
-            )
-            nc.vector.scalar_tensor_tensor(
-                out=mix[:], in0=mix[:], scalar=rstd_h[:, 0:1], in1=lnh_b_all[:],
-                op0=ALU.mult, op1=ALU.add,
-            )
-            nc.sync.dma_start(out=out[m * P : (m + 1) * P, :], in_=mix[:])
-
-        ig_of = {}
-        sg_of = {}
-
-        def input_gates_first_half(m):
-            ig, neg_mean = input_product(m)
-            ig_of[m] = (ig, input_centre(ig, neg_mean))
-
-        input_gates_first_half(0)
-        quantise_states()
-        input_gates_first_half(1)
-        input_bias(*ig_of[0])
-        sg_of[0] = state_product(0)
-        input_bias(*ig_of[1])
-        rstd_of = {0: state_centre(*sg_of[0])}
-        for m in range(BATCH_TILES):
-            if m + 1 < BATCH_TILES:
-                sg_of[m + 1] = state_product(m + 1)
-            finish(m, ig_of[m][0], sg_of[m][0], rstd_of[m], nc.vector if m == BATCH_TILES - 1 else nc.gpsimd)
-            if m + 2 < BATCH_TILES:
-                input_gates_first_half(m + 2)
-            if m + 1 < BATCH_TILES:
-                rstd_of[m + 1] = state_centre(*sg_of[m + 1])
-            if m + 2 < BATCH_TILES:
-                input_bias(*ig_of[m + 2])
+        state_steps = 32
+        for k in range(n_matrices + state_steps // BANKS_PER_ROW):
+            for n in range(BANKS_PER_ROW):
+                if k < n_matrices:
+                    sweep_step(k, n)
+                if k < n_matrices and k % 2 == 0 and n == 3:
+                    quantise_states(k // 2)
+                if k % 2 == 1 and k - 1 < n_matrices:
+                    input_step((k - 1) // 2, n)
+                for m in range(BATCH_TILES):
+                    t = (k - (2 * m + 2)) * BANKS_PER_ROW + n
+                    if 0 <= t < state_steps:
+                        state_step(m, t)

@@ -251,11 +251,13 @@ def tile_lngru2dcell_kernel(
             )
 
         def input_step(m, n):
-            if n % 2 == 0:
-                block = slice(n * BANK, (n + 2) * BANK)
+            if n < 4:
+                block = slice(n * STATE, (n + 1) * STATE)
                 centre_and_gain(2 * m, block, lni_g_all[:, block])
-            in_cand = CAND_FIRST <= n * BANK < CAND_FIRST + STATE
-            scale_and_bias(2 * m, bank_cols(n), PICK_LNI_B if in_cand else PICK_BOTH_B)
+            else:
+                for bank in (2 * (n - 4), 2 * (n - 4) + 1):
+                    in_cand = CAND_FIRST <= bank * BANK < CAND_FIRST + STATE
+                    scale_and_bias(2 * m, bank_cols(bank), PICK_LNI_B if in_cand else PICK_BOTH_B)
 
         mix_of = {}
         last_norm_of = {}
@@ -269,52 +271,53 @@ def tile_lngru2dcell_kernel(
             p1 = p1_sb[:, m, :]
             rstd = norm_of[2 * m + 1][1]
             helper = nc.vector if m == BATCH_TILES - 1 else nc.gpsimd
-            if t == 0:
-                mix_of[m] = blend.tile([P, STATE], F32, name="mix")
-                nc.gpsimd.tensor_tensor(out=mix_of[m][:], in0=p0, in1=p1, op=ALU.subtract)
-            mix = mix_of[m]
-            if t < 8 and t % 2 == 0:
-                centre_and_gain(2 * m + 1, block_order[t // 2], lns_g_banks[gain_bank_of_block[t // 2]][:])
-            if t == 3:
+            if t < 4:
+                centre_and_gain(2 * m + 1, block_order[t], lns_g_banks[gain_bank_of_block[t]][:])
+            if t == 4:
                 for h in range(2):
                     scale_and_bias(2 * m + 1, bank_cols(CAND_FIRST // BANK + h), PICK_LNS_B)
-            if t in (1, 5, 7):
-                block = block_order[t // 2]
+                mix_of[m] = blend.tile([P, STATE], F32, name="mix")
+                helper.tensor_tensor(out=mix_of[m][:], in0=p0, in1=p1, op=ALU.subtract)
+            if t in (5, 6, 7):
+                block = (RESET, LERP, INPUT)[t - 5]
                 nc.vector.scalar_tensor_tensor(
                     out=sg[:, block], in0=sg[:, block], scalar=rstd[:, 0:1], in1=ig[:, block],
                     op0=ALU.mult, op1=ALU.add,
                 )
-            if t == 3:
-                nc.scalar.activation(out=sg[:, RESET], in_=sg[:, RESET], func=ACT.Sigmoid, scale=-1.0)
-            if t == 5:
-                helper.tensor_tensor(out=sg[:, CAND], in0=sg[:, CAND], in1=sg[:, RESET], op=ALU.mult)
-                helper.tensor_tensor(out=sg[:, CAND], in0=sg[:, CAND], in1=ig[:, CAND], op=ALU.add)
             if t == 7:
-                nc.scalar.activation(out=sg[:, LERP], in_=sg[:, LERP], func=ACT.Sigmoid)
+                nc.scalar.activation(out=sg[:, RESET], in_=sg[:, RESET], func=ACT.Sigmoid, scale=-1.0)
             if t == 8:
-                nc.gpsimd.tensor_tensor(out=mix[:], in0=mix[:], in1=sg[:, LERP], op=ALU.mult)
-                nc.gpsimd.tensor_tensor(out=mix[:], in0=mix[:], in1=p1, op=ALU.add)
+                nc.scalar.activation(out=sg[:, LERP], in_=sg[:, LERP], func=ACT.Sigmoid)
             if t == 9:
                 nc.scalar.activation(out=sg[:, INPUT], in_=sg[:, INPUT], func=ACT.Sigmoid)
+            if t == 9:
+                nc.vector.tensor_tensor(out=sg[:, CAND], in0=sg[:, CAND], in1=sg[:, RESET], op=ALU.mult)
             if t == 10:
+                nc.vector.tensor_tensor(out=sg[:, CAND], in0=sg[:, CAND], in1=ig[:, CAND], op=ALU.add)
+            if t == 12:
                 nc.scalar.activation(out=sg[:, CAND], in_=sg[:, CAND], func=ACT.Tanh)
-            if t == 11:
+                mix = mix_of[m]
+                helper.tensor_tensor(out=mix[:], in0=mix[:], in1=sg[:, LERP], op=ALU.mult)
+                helper.tensor_tensor(out=mix[:], in0=mix[:], in1=p1, op=ALU.add)
                 helper.tensor_tensor(out=mix[:], in0=mix[:], in1=sg[:, CAND], op=ALU.subtract)
                 helper.tensor_tensor(out=mix[:], in0=mix[:], in1=sg[:, INPUT], op=ALU.mult)
                 helper.tensor_tensor(out=mix[:], in0=mix[:], in1=sg[:, CAND], op=ALU.add)
-            if t == 24:
+            if t == 23:
+                mix = mix_of[m]
                 chunk_stats = stat.tile([P, 2, 6], F32)
                 for h in range(2):
                     nc.vector.bn_stats(out=chunk_stats[:, h, :], in_=mix[:, bank_cols(h)])
                 mean_var = stat.tile([P, 2], F32)
                 nc.vector.bn_aggr(out=mean_var[:], in_=chunk_stats[:].rearrange("p a b -> p (a b)"))
                 last_norm_of[m] = (mean_var, rsqrt(mean_var[:, 1:2]))
-            if t == 26:
+            if t == 30:
+                mix = mix_of[m]
                 nc.vector.scalar_tensor_tensor(
                     out=mix[:], in0=mix[:], scalar=last_norm_of[m][0][:, 0:1], in1=lnh_g_all[:],
                     op0=ALU.subtract, op1=ALU.mult,
                 )
-            if t == 28:
+            if t == 31:
+                mix = mix_of[m]
                 nc.vector.scalar_tensor_tensor(
                     out=mix[:], in0=mix[:], scalar=last_norm_of[m][1][:, 0:1], in1=lnh_b_all[:],
                     op0=ALU.mult, op1=ALU.add,
@@ -328,9 +331,9 @@ def tile_lngru2dcell_kernel(
                     sweep_step(k, n)
                 if k < n_matrices and k % 2 == 0 and n == 3:
                     quantise_states(k // 2)
-                if k % 2 == 1 and k - 1 < n_matrices:
-                    input_step((k - 1) // 2, n)
                 for m in range(BATCH_TILES):
                     t = (k - (2 * m + 2)) * BANKS_PER_ROW + n
                     if 0 <= t < state_steps:
                         state_step(m, t)
+                if k % 2 == 1 and k - 1 < n_matrices:
+                    input_step((k - 1) // 2, n)

@@ -31,7 +31,8 @@ CAND_FIRST = 2 * STATE
 CAND = slice(CAND_FIRST, CAND_FIRST + STATE)
 LERP = slice(3 * STATE, 4 * STATE)
 
-ROW_LNS_G, ROW_LNI_B, ROW_LNS_B = 0, 32, 64
+ROW_LNS_G, ROW_LNI_B, ROW_LNS_B, ROW_LNI_G = 0, 32, 64, 96
+ROW_LNH_G, ROW_LNH_B = 0, 32
 
 FLOPS = 2 * BATCH * GATES * (D_IN + 2 * STATE)
 
@@ -62,15 +63,16 @@ def tile_lngru2dcell_kernel(
         act_codes = keep.tile([P, n_operands, P], U32, align_bytes=64)
         act_scales = keep.tile([P, n_operands, P], U8, align_bytes=64)
         rows = keep.tile([P, GATES], BF16)
+        rows_h = keep.tile([P, STATE], BF16)
         lni_g_all = keep.tile([P, GATES], BF16)
         lnh_g_all = keep.tile([P, STATE], BF16)
         lnh_b_all = keep.tile([P, STATE], BF16)
         ident = keep.tile([P, P], F32)
-        pick = keep.tile([P, 4, P], BF16)
+        pick = keep.tile([P, 5, P], BF16)
         neg_half = keep.tile([P, 1], F32)
         zero_col = keep.tile([P, 1], F32)
         warm_col = keep.tile([P, 1], F32)
-        squares = keep.tile([P, BANK], F32)
+        squares = keep.tile([P, 2 * BANK], F32)
         ig_tiles = [keep.tile([P, GATES], F32, name="ig%d" % i) for i in range(2)]
         sg_tiles = [keep.tile([P, GATES], F32, name="sg%d" % i) for i in range(2)]
 
@@ -79,13 +81,15 @@ def tile_lngru2dcell_kernel(
         nc.vector.memset(zero_col[:], 0.0)
         nc.vector.memset(neg_half[:], -0.5)
         nc.vector.memset(rows[:].bitcast(I32), 0)
+        nc.vector.memset(rows_h[:].bitcast(I32), 0)
         nc.vector.memset(pick[:], 0.0)
-        PICK_LNS_G, PICK_BOTH_B, PICK_LNI_B, PICK_LNS_B = 0, 1, 2, 3
-        nc.vector.memset(pick[ROW_LNS_G : ROW_LNS_G + 1, PICK_LNS_G, :], 1.0)
+        for j in range(4):
+            nc.vector.memset(pick[32 * j : 32 * j + 1, j, :], 1.0)
+        PICK_BOTH_B = 4
         nc.vector.memset(pick[ROW_LNI_B : ROW_LNI_B + 1, PICK_BOTH_B, :], 1.0)
         nc.vector.memset(pick[ROW_LNS_B : ROW_LNS_B + 1, PICK_BOTH_B, :], 1.0)
-        nc.vector.memset(pick[ROW_LNI_B : ROW_LNI_B + 1, PICK_LNI_B, :], 1.0)
-        nc.vector.memset(pick[ROW_LNS_B : ROW_LNS_B + 1, PICK_LNS_B, :], 1.0)
+        PICK_LNS_G, PICK_LNI_B, PICK_LNS_B, PICK_LNI_G = ROW_LNS_G // 32, ROW_LNI_B // 32, ROW_LNS_B // 32, ROW_LNI_G // 32
+        PICK_LNH_G, PICK_LNH_B = ROW_LNH_G // 32, ROW_LNH_B // 32
         make_identity(nc, ident[:])
         nc.scalar.activation(out=warm_col[:], in_=zero_col[:], func=ACT.Sigmoid)
 
@@ -111,13 +115,13 @@ def tile_lngru2dcell_kernel(
         nc.scalar.dma_start(out=rows[ROW_LNS_G : ROW_LNS_G + 1, :], in_=lns_g.unsqueeze(0))
         nc.scalar.dma_start(out=rows[ROW_LNI_B : ROW_LNI_B + 1, :], in_=lni_b.unsqueeze(0))
         nc.scalar.dma_start(out=rows[ROW_LNS_B : ROW_LNS_B + 1, :], in_=lns_b.unsqueeze(0))
-        nc.scalar.dma_start(out=lni_g_all[:], in_=lni_g.partition_broadcast(P))
+        nc.scalar.dma_start(out=rows[ROW_LNI_G : ROW_LNI_G + 1, :], in_=lni_g.unsqueeze(0))
+        nc.scalar.dma_start(out=rows_h[ROW_LNH_G : ROW_LNH_G + 1, :], in_=lnh_g.unsqueeze(0))
+        nc.scalar.dma_start(out=rows_h[ROW_LNH_B : ROW_LNH_B + 1, :], in_=lnh_b.unsqueeze(0))
         nc.scalar.dma_start(out=p0_sb[:], in_=s_prev0.rearrange("(m p) d -> p m d", p=P))
         nc.scalar.dma_start(out=p1_sb[:], in_=s_prev1.rearrange("(m p) d -> p m d", p=P))
-        nc.scalar.dma_start(out=lnh_g_all[:], in_=lnh_g.partition_broadcast(P))
-        nc.scalar.dma_start(out=lnh_b_all[:], in_=lnh_b.partition_broadcast(P))
 
-        def quantise_round(first_operand, sources):
+        def quantise_round(first_operand, sources, scalar_helps):
             grouped = stage.tile([P, ROUND, P, PACK], BF16, align_bytes=64)
             grouped_words = grouped[:].rearrange("p c b t -> p (c b t)").bitcast(F32)
             for half in range(2):
@@ -130,10 +134,10 @@ def tile_lngru2dcell_kernel(
                 dst = grouped_words[:, half * BANK : (half + 1) * BANK]
                 dst = dst.rearrange("p (c b u) -> p c b u", c=2, u=2)
                 src = flipped[:].rearrange("p (c u) b -> p c b u", u=2)
-                if half == 0:
-                    nc.vector.tensor_copy(out=dst, in_=src)
-                else:
+                if half == 1 and scalar_helps:
                     nc.scalar.copy(out=dst, in_=src)
+                else:
+                    nc.vector.tensor_copy(out=dst, in_=src)
             taken = slice(first_operand, first_operand + ROUND)
             nc.vector.quantize_mx(
                 out=act_codes[:, taken, :].rearrange("p c b -> p (c b)").bitcast(FP8X4),
@@ -141,7 +145,7 @@ def tile_lngru2dcell_kernel(
                 in_=grouped[:].rearrange("p c b t -> p (c b t)"),
             )
 
-        quantise_round(0, [x_sb[:, m, :].bitcast(F32) for m in range(BATCH_TILES)])
+        quantise_round(0, [x_sb[:, m, :].bitcast(F32) for m in range(BATCH_TILES)], True)
 
         lns_g_banks = []
         for c in range(4):
@@ -163,15 +167,18 @@ def tile_lngru2dcell_kernel(
                 BATCH_TILES + STATE_PASSES * m,
                 [p0_words[:, 0:WORDS], p0_words[:, WORDS : 2 * WORDS],
                  p1_words[:, 0:WORDS], p1_words[:, WORDS : 2 * WORDS]],
+                False,
             )
 
         def bank_cols(n):
             return slice(n * BANK, (n + 1) * BANK)
 
-        def row_total(parts, factor):
+        def row_total(parts, width, factor):
             scaled = stat.tile([P, BANKS_PER_ROW], F32)
             total = stat.tile([P, 1], F32)
-            nc.scalar.activation(out=scaled[:], in_=parts[:], func=ACT.Copy, scale=factor, accum_out=total[:])
+            nc.scalar.activation(
+                out=scaled[:, 0:width], in_=parts[:], func=ACT.Copy, scale=factor, accum_out=total[:]
+            )
             return total
 
         def rsqrt(variance):
@@ -201,7 +208,7 @@ def tile_lngru2dcell_kernel(
             cols = bank_cols(n)
             if n == 0:
                 bank_sums = stat.tile([P, BANKS_PER_ROW], F32)
-                bank_squares = stat.tile([P, BANKS_PER_ROW], F32)
+                bank_squares = stat.tile([P, BANKS_PER_ROW // 2], F32)
                 neg_shift = stat.tile([P, 1], F32)
                 sums_of[matrix] = (bank_sums, bank_squares, neg_shift)
             bank_sums, bank_squares, neg_shift = sums_of[matrix]
@@ -219,13 +226,14 @@ def tile_lngru2dcell_kernel(
             nc.scalar.activation(out=raw[:, cols], in_=acc[:], func=ACT.Copy, accum_out=bank_sums[:, n : n + 1])
             if n == 0:
                 nc.scalar.mul(out=neg_shift[:], in_=bank_sums[:, 0:1], mul=-1.0 / BANK)
-            nc.scalar.activation(
-                out=squares[:], in_=raw[:, cols], func=ACT.Square, bias=neg_shift[:, 0:1], scale=1.0,
-                accum_out=bank_squares[:, n : n + 1],
-            )
+            if n % 2 == 1:
+                nc.scalar.activation(
+                    out=squares[:], in_=raw[:, (n - 1) * BANK : (n + 1) * BANK], func=ACT.Square,
+                    bias=neg_shift[:, 0:1], scale=1.0, accum_out=bank_squares[:, n // 2 : n // 2 + 1],
+                )
             if n == BANKS_PER_ROW - 1:
-                neg_mean = row_total(bank_sums, -1.0 / GATES)
-                mean_square = row_total(bank_squares, 1.0 / GATES)
+                neg_mean = row_total(bank_sums, BANKS_PER_ROW, -1.0 / GATES)
+                mean_square = row_total(bank_squares, BANKS_PER_ROW // 2, 1.0 / GATES)
                 offset_square = stat.tile([P, 1], F32)
                 nc.scalar.activation(
                     out=offset_square[:], in_=neg_mean[:], func=ACT.Square, bias=neg_shift[:, 0:1], scale=-1.0
@@ -249,6 +257,19 @@ def tile_lngru2dcell_kernel(
                 out=raw[:, cols], in0=raw[:, cols], scalar=norm_of[matrix][1][:, 0:1], in1=bias[:],
                 op0=ALU.mult, op1=ALU.add,
             )
+
+        def spread(source, picked, cols, dest):
+            repeated = psum_bias.tile([P, BANK], F32, tag="bias")
+            nc.tensor.matmul(out=repeated[:], lhsT=pick[:, picked, :], rhs=source[:, cols], start=True, stop=True)
+            nc.vector.tensor_copy(out=dest[:, cols], in_=repeated[:])
+
+        def prepare_step(n):
+            spread(rows, PICK_LNI_G, bank_cols(n), lni_g_all)
+            if n < 2:
+                spread(rows_h, PICK_LNH_G, bank_cols(n), lnh_g_all)
+                spread(rows_h, PICK_LNH_B, bank_cols(n), lnh_b_all)
+            if n >= BANKS_PER_ROW - BATCH_TILES:
+                quantise_states(n - (BANKS_PER_ROW - BATCH_TILES))
 
         def input_step(m, n):
             if n < 4:
@@ -329,8 +350,8 @@ def tile_lngru2dcell_kernel(
             for n in range(BANKS_PER_ROW):
                 if k < n_matrices:
                     sweep_step(k, n)
-                if k < n_matrices and k % 2 == 0 and n == 3:
-                    quantise_states(k // 2)
+                if k == 0:
+                    prepare_step(n)
                 for m in range(BATCH_TILES):
                     t = (k - (2 * m + 2)) * BANKS_PER_ROW + n
                     if 0 <= t < state_steps:

@@ -31,8 +31,8 @@ CAND_FIRST = 2 * STATE
 CAND = slice(CAND_FIRST, CAND_FIRST + STATE)
 LERP = slice(3 * STATE, 4 * STATE)
 
-ROW_LNS_G, ROW_LNI_B, ROW_LNS_B, ROW_LNI_G = 0, 32, 64, 96
-ROW_LNH_G, ROW_LNH_B = 0, 32
+ROW_LNS_G, ROW_LNI_B, ROW_LNS_B = 0, 32, 64
+COL_LNI_G, COL_LNH_G, COL_LNH_B = 0, GATES // P, GATES // P + STATE // P
 
 FLOPS = 2 * BATCH * GATES * (D_IN + 2 * STATE)
 
@@ -63,12 +63,11 @@ def tile_lngru2dcell_kernel(
         act_codes = keep.tile([P, n_operands, P], U32, align_bytes=64)
         act_scales = keep.tile([P, n_operands, P], U8, align_bytes=64)
         rows = keep.tile([P, GATES], BF16)
-        rows_h = keep.tile([P, STATE], BF16)
-        lni_g_all = keep.tile([P, GATES], BF16)
-        lnh_g_all = keep.tile([P, STATE], BF16)
-        lnh_b_all = keep.tile([P, STATE], BF16)
+        vec_rows = keep.tile([P, P], BF16)
+        vec_cols = keep.tile([P, P], BF16)
         ident = keep.tile([P, P], F32)
-        pick = keep.tile([P, 5, P], BF16)
+        ident_bf = keep.tile([P, P], BF16)
+        pick = keep.tile([P, 4, P], BF16)
         neg_half = keep.tile([P, 1], F32)
         zero_col = keep.tile([P, 1], F32)
         warm_col = keep.tile([P, 1], F32)
@@ -81,16 +80,16 @@ def tile_lngru2dcell_kernel(
         nc.vector.memset(zero_col[:], 0.0)
         nc.vector.memset(neg_half[:], -0.5)
         nc.vector.memset(rows[:].bitcast(I32), 0)
-        nc.vector.memset(rows_h[:].bitcast(I32), 0)
+        nc.vector.memset(vec_rows[:].bitcast(I32), 0)
         nc.vector.memset(pick[:], 0.0)
-        for j in range(4):
-            nc.vector.memset(pick[32 * j : 32 * j + 1, j, :], 1.0)
-        PICK_BOTH_B = 4
+        PICK_LNS_G, PICK_BOTH_B, PICK_LNI_B, PICK_LNS_B = 0, 1, 2, 3
+        nc.vector.memset(pick[ROW_LNS_G : ROW_LNS_G + 1, PICK_LNS_G, :], 1.0)
         nc.vector.memset(pick[ROW_LNI_B : ROW_LNI_B + 1, PICK_BOTH_B, :], 1.0)
         nc.vector.memset(pick[ROW_LNS_B : ROW_LNS_B + 1, PICK_BOTH_B, :], 1.0)
-        PICK_LNS_G, PICK_LNI_B, PICK_LNS_B, PICK_LNI_G = ROW_LNS_G // 32, ROW_LNI_B // 32, ROW_LNS_B // 32, ROW_LNI_G // 32
-        PICK_LNH_G, PICK_LNH_B = ROW_LNH_G // 32, ROW_LNH_B // 32
+        nc.vector.memset(pick[ROW_LNI_B : ROW_LNI_B + 1, PICK_LNI_B, :], 1.0)
+        nc.vector.memset(pick[ROW_LNS_B : ROW_LNS_B + 1, PICK_LNS_B, :], 1.0)
         make_identity(nc, ident[:])
+        make_identity(nc, ident_bf[:])
         nc.scalar.activation(out=warm_col[:], in_=zero_col[:], func=ACT.Sigmoid)
 
         nc.sync.dma_start(out=x_sb[:], in_=x.rearrange("(m p) d -> p m d", p=P))
@@ -115,9 +114,10 @@ def tile_lngru2dcell_kernel(
         nc.scalar.dma_start(out=rows[ROW_LNS_G : ROW_LNS_G + 1, :], in_=lns_g.unsqueeze(0))
         nc.scalar.dma_start(out=rows[ROW_LNI_B : ROW_LNI_B + 1, :], in_=lni_b.unsqueeze(0))
         nc.scalar.dma_start(out=rows[ROW_LNS_B : ROW_LNS_B + 1, :], in_=lns_b.unsqueeze(0))
-        nc.scalar.dma_start(out=rows[ROW_LNI_G : ROW_LNI_G + 1, :], in_=lni_g.unsqueeze(0))
-        nc.scalar.dma_start(out=rows_h[ROW_LNH_G : ROW_LNH_G + 1, :], in_=lnh_g.unsqueeze(0))
-        nc.scalar.dma_start(out=rows_h[ROW_LNH_B : ROW_LNH_B + 1, :], in_=lnh_b.unsqueeze(0))
+        for vector, col, length in ((lni_g, COL_LNI_G, GATES), (lnh_g, COL_LNH_G, STATE), (lnh_b, COL_LNH_B, STATE)):
+            nc.scalar.dma_start(
+                out=vec_rows[col : col + length // P, :], in_=vector.rearrange("(c p) -> c p", p=P)
+            )
         nc.scalar.dma_start(out=p0_sb[:], in_=s_prev0.rearrange("(m p) d -> p m d", p=P))
         nc.scalar.dma_start(out=p1_sb[:], in_=s_prev1.rearrange("(m p) d -> p m d", p=P))
 
@@ -159,6 +159,20 @@ def tile_lngru2dcell_kernel(
                     stop=True,
                 )
             lns_g_banks.append(gain)
+
+        flipped_rows = psum_bias.tile([P, P], BF16, tag="bias")
+        nc.tensor.transpose(flipped_rows[:], vec_rows[:], ident_bf[:])
+        nc.vector.tensor_copy(out=vec_cols[:], in_=flipped_rows[:])
+
+        def repeat(first_col):
+            bank = psum_bias.tile([P, STATE], BF16, tag="bias")
+            for j in range(STATE // P):
+                nc.tensor.transpose(
+                    bank[:, j * P : (j + 1) * P],
+                    vec_cols[:, first_col + j : first_col + j + 1].to_broadcast([P, P]),
+                    ident_bf[:],
+                )
+            return bank
 
         def quantise_states(m):
             p0_words = p0_sb[:, m, :].bitcast(F32)
@@ -258,23 +272,14 @@ def tile_lngru2dcell_kernel(
                 op0=ALU.mult, op1=ALU.add,
             )
 
-        def spread(source, picked, cols, dest):
-            repeated = psum_bias.tile([P, BANK], F32, tag="bias")
-            nc.tensor.matmul(out=repeated[:], lhsT=pick[:, picked, :], rhs=source[:, cols], start=True, stop=True)
-            nc.vector.tensor_copy(out=dest[:, cols], in_=repeated[:])
-
         def prepare_step(n):
-            spread(rows, PICK_LNI_G, bank_cols(n), lni_g_all)
-            if n < 2:
-                spread(rows_h, PICK_LNH_G, bank_cols(n), lnh_g_all)
-                spread(rows_h, PICK_LNH_B, bank_cols(n), lnh_b_all)
             if n >= BANKS_PER_ROW - BATCH_TILES:
                 quantise_states(n - (BANKS_PER_ROW - BATCH_TILES))
 
         def input_step(m, n):
             if n < 4:
                 block = slice(n * STATE, (n + 1) * STATE)
-                centre_and_gain(2 * m, block, lni_g_all[:, block])
+                centre_and_gain(2 * m, block, repeat(COL_LNI_G + n * (STATE // P))[:])
             else:
                 for bank in (2 * (n - 4), 2 * (n - 4) + 1):
                     in_cand = CAND_FIRST <= bank * BANK < CAND_FIRST + STATE
@@ -312,9 +317,8 @@ def tile_lngru2dcell_kernel(
             if t == 9:
                 nc.scalar.activation(out=sg[:, INPUT], in_=sg[:, INPUT], func=ACT.Sigmoid)
             if t == 9:
-                nc.vector.tensor_tensor(out=sg[:, CAND], in0=sg[:, CAND], in1=sg[:, RESET], op=ALU.mult)
-            if t == 10:
-                nc.vector.tensor_tensor(out=sg[:, CAND], in0=sg[:, CAND], in1=ig[:, CAND], op=ALU.add)
+                helper.tensor_tensor(out=sg[:, CAND], in0=sg[:, CAND], in1=sg[:, RESET], op=ALU.mult)
+                helper.tensor_tensor(out=sg[:, CAND], in0=sg[:, CAND], in1=ig[:, CAND], op=ALU.add)
             if t == 12:
                 nc.scalar.activation(out=sg[:, CAND], in_=sg[:, CAND], func=ACT.Tanh)
                 mix = mix_of[m]
@@ -334,13 +338,13 @@ def tile_lngru2dcell_kernel(
             if t == 30:
                 mix = mix_of[m]
                 nc.vector.scalar_tensor_tensor(
-                    out=mix[:], in0=mix[:], scalar=last_norm_of[m][0][:, 0:1], in1=lnh_g_all[:],
+                    out=mix[:], in0=mix[:], scalar=last_norm_of[m][0][:, 0:1], in1=repeat(COL_LNH_G)[:],
                     op0=ALU.subtract, op1=ALU.mult,
                 )
             if t == 31:
                 mix = mix_of[m]
                 nc.vector.scalar_tensor_tensor(
-                    out=mix[:], in0=mix[:], scalar=last_norm_of[m][1][:, 0:1], in1=lnh_b_all[:],
+                    out=mix[:], in0=mix[:], scalar=last_norm_of[m][1][:, 0:1], in1=repeat(COL_LNH_B)[:],
                     op0=ALU.mult, op1=ALU.add,
                 )
                 nc.sync.dma_start(out=out[m * P : (m + 1) * P, :], in_=mix[:])

@@ -45,7 +45,7 @@ def tile_lngru2dcell_kernel(
     with ExitStack() as ctx:
         keep = ctx.enter_context(tc.tile_pool(name="keep", bufs=1))
         stage = ctx.enter_context(tc.tile_pool(name="stage", bufs=2))
-        blend = ctx.enter_context(tc.tile_pool(name="blend", bufs=2))
+        blend = ctx.enter_context(tc.tile_pool(name="blend", bufs=3))
         stat = ctx.enter_context(tc.tile_pool(name="stat", bufs=4))
         psum_gain = ctx.enter_context(tc.psum_pool(name="psum_gain", bufs=1))
         psum_acc = ctx.enter_context(tc.psum_pool(name="psum_acc", bufs=2))
@@ -72,7 +72,7 @@ def tile_lngru2dcell_kernel(
         zero_col = keep.tile([P, 1], F32)
         warm_col = keep.tile([P, 1], F32)
         squares = keep.tile([P, 2 * BANK], F32)
-        ig_tiles = [keep.tile([P, GATES], F32, name="ig%d" % i) for i in range(2)]
+        ig_tiles = [keep.tile([P, GATES], F32, name="ig%d" % i) for i in range(3)]
         sg_tiles = [keep.tile([P, GATES], F32, name="sg%d" % i) for i in range(2)]
 
         nc.vector.memset(wi_plane[:].bitcast(I32), 0)
@@ -93,6 +93,13 @@ def tile_lngru2dcell_kernel(
         nc.scalar.activation(out=warm_col[:], in_=zero_col[:], func=ACT.Sigmoid)
 
         nc.sync.dma_start(out=x_sb[:], in_=x.rearrange("(m p) d -> p m d", p=P))
+        nc.sync.dma_start(out=rows[ROW_LNS_G : ROW_LNS_G + 1, :], in_=lns_g.unsqueeze(0))
+        nc.sync.dma_start(out=rows[ROW_LNI_B : ROW_LNI_B + 1, :], in_=lni_b.unsqueeze(0))
+        nc.sync.dma_start(out=rows[ROW_LNS_B : ROW_LNS_B + 1, :], in_=lns_b.unsqueeze(0))
+        for vector, col, length in ((lni_g, COL_LNI_G, GATES), (lnh_g, COL_LNH_G, STATE), (lnh_b, COL_LNH_B, STATE)):
+            nc.sync.dma_start(
+                out=vec_rows[col : col + length // P, :], in_=vector.rearrange("(c p) -> c p", p=P)
+            )
         for quad in range(4):
             nc.sync.dma_start(
                 out=wi_plane[32 * quad : 32 * quad + 4, :].bitcast(I32),
@@ -102,6 +109,8 @@ def tile_lngru2dcell_kernel(
         for c in range(4):
             cols = slice(c * STATE, (c + 1) * STATE)
             nc.sync.dma_start(out=wi_words[:, cols].bitcast(I32), in_=wi_dram[:, cols])
+        nc.sync.dma_start(out=p0_sb[:], in_=s_prev0.rearrange("(m p) d -> p m d", p=P))
+        nc.sync.dma_start(out=p1_sb[:], in_=s_prev1.rearrange("(m p) d -> p m d", p=P))
         for quad in range(4):
             nc.sync.dma_start(
                 out=ws_planes[32 * quad : 32 * quad + 16, :].bitcast(I32),
@@ -111,15 +120,6 @@ def tile_lngru2dcell_kernel(
         for n in range(BANKS_PER_ROW):
             cols = slice(n * BANK, (n + 1) * BANK)
             nc.sync.dma_start(out=ws_words[:, :, cols].bitcast(I32), in_=ws_dram[:, :, cols])
-        nc.scalar.dma_start(out=rows[ROW_LNS_G : ROW_LNS_G + 1, :], in_=lns_g.unsqueeze(0))
-        nc.scalar.dma_start(out=rows[ROW_LNI_B : ROW_LNI_B + 1, :], in_=lni_b.unsqueeze(0))
-        nc.scalar.dma_start(out=rows[ROW_LNS_B : ROW_LNS_B + 1, :], in_=lns_b.unsqueeze(0))
-        for vector, col, length in ((lni_g, COL_LNI_G, GATES), (lnh_g, COL_LNH_G, STATE), (lnh_b, COL_LNH_B, STATE)):
-            nc.scalar.dma_start(
-                out=vec_rows[col : col + length // P, :], in_=vector.rearrange("(c p) -> c p", p=P)
-            )
-        nc.scalar.dma_start(out=p0_sb[:], in_=s_prev0.rearrange("(m p) d -> p m d", p=P))
-        nc.scalar.dma_start(out=p1_sb[:], in_=s_prev1.rearrange("(m p) d -> p m d", p=P))
 
         def quantise_round(first_operand, sources, scalar_helps):
             grouped = stage.tile([P, ROUND, P, PACK], BF16, align_bytes=64)
@@ -209,7 +209,19 @@ def tile_lngru2dcell_kernel(
         norm_of = {}
 
         def raw_tile(matrix):
-            return (sg_tiles if matrix % 2 else ig_tiles)[(matrix // 2) % 2]
+            m = matrix // 2
+            return sg_tiles[m % 2] if matrix % 2 else ig_tiles[m % 3]
+
+        first_chunks = stat.tile([P, BANKS_PER_ROW, 6], F32)
+
+        def first_statistics(n, values):
+            nc.vector.bn_stats(out=first_chunks[:, n, :], in_=values)
+            if n == BANKS_PER_ROW - 1:
+                first_mean_var = stat.tile([P, 2], F32)
+                nc.vector.bn_aggr(out=first_mean_var[:], in_=first_chunks[:].rearrange("p a b -> p (a b)"))
+                first_neg_mean = stat.tile([P, 1], F32)
+                nc.scalar.mul(out=first_neg_mean[:], in_=first_mean_var[:, 0:1], mul=-1.0)
+                norm_of[0] = (first_neg_mean, rsqrt(first_mean_var[:, 1:2]))
 
         def sweep_step(matrix, n):
             m = matrix // 2
@@ -237,6 +249,10 @@ def tile_lngru2dcell_kernel(
                     start=(j == 0),
                     stop=(j == len(passes) - 1),
                 )
+            if matrix == 0:
+                nc.scalar.copy(out=raw[:, cols], in_=acc[:])
+                first_statistics(n, raw[:, cols])
+                return
             nc.scalar.activation(out=raw[:, cols], in_=acc[:], func=ACT.Copy, accum_out=bank_sums[:, n : n + 1])
             if n == 0:
                 nc.scalar.mul(out=neg_shift[:], in_=bank_sums[:, 0:1], mul=-1.0 / BANK)
@@ -272,10 +288,6 @@ def tile_lngru2dcell_kernel(
                 op0=ALU.mult, op1=ALU.add,
             )
 
-        def prepare_step(n):
-            if n >= BANKS_PER_ROW - BATCH_TILES:
-                quantise_states(n - (BANKS_PER_ROW - BATCH_TILES))
-
         def input_step(m, n):
             if n < 4:
                 block = slice(n * STATE, (n + 1) * STATE)
@@ -291,7 +303,7 @@ def tile_lngru2dcell_kernel(
         gain_bank_of_block = [0, 2, 3, 1]
 
         def state_step(m, t):
-            ig = ig_tiles[m % 2]
+            ig = ig_tiles[m % 3]
             sg = sg_tiles[m % 2]
             p0 = p0_sb[:, m, :]
             p1 = p1_sb[:, m, :]
@@ -349,16 +361,17 @@ def tile_lngru2dcell_kernel(
                 )
                 nc.sync.dma_start(out=out[m * P : (m + 1) * P, :], in_=mix[:])
 
+        sweep_order = [0, 2, 1, 4, 3, 6, 5, 7]
         state_steps = 32
         for k in range(n_matrices + state_steps // BANKS_PER_ROW):
             for n in range(BANKS_PER_ROW):
                 if k < n_matrices:
-                    sweep_step(k, n)
-                if k == 0:
-                    prepare_step(n)
+                    sweep_step(sweep_order[k], n)
                 for m in range(BATCH_TILES):
-                    t = (k - (2 * m + 2)) * BANKS_PER_ROW + n
+                    t = (k - sweep_order.index(2 * m + 1) - 1) * BANKS_PER_ROW + n
                     if 0 <= t < state_steps:
                         state_step(m, t)
-                if k % 2 == 1 and k - 1 < n_matrices:
-                    input_step((k - 1) // 2, n)
+                    if k == sweep_order.index(2 * m) + 1:
+                        input_step(m, n)
+            if k < BATCH_TILES:
+                quantise_states(k)

from contextlib import ExitStack

import concourse.mybir as mybir
from concourse.masks import make_identity

BF16 = mybir.dt.bfloat16
F32 = mybir.dt.float32
I32 = mybir.dt.int32
U32 = mybir.dt.uint32
U8 = mybir.dt.uint8
FP8X4 = mybir.dt.float8_e4m3fn_x4
ALU = mybir.AluOpType
ACT = mybir.ActivationFunctionType

P = 128
PACK = 4
K_PASS = P * PACK
BATCH, D_IN, STATE = 512, 512, 1024
GATES = 4 * STATE
EPS = 1e-5
BATCH_TILES = BATCH // P
BANK = 512
BANKS_PER_ROW = GATES // BANK
STATE_PASSES = 2 * STATE // K_PASS
WORDS = K_PASS // 2
ROUND = 4

RESET = slice(0 * STATE, 1 * STATE)
INPUT = slice(1 * STATE, 2 * STATE)
CAND_FIRST = 2 * STATE
CAND = slice(CAND_FIRST, CAND_FIRST + STATE)
LERP = slice(3 * STATE, 4 * STATE)

ROW_LNS_G, ROW_LNI_B, ROW_LNS_B = 0, 32, 64
COL_LNI_G, COL_LNH_G, COL_LNH_B = 0, GATES // P, GATES // P + STATE // P

FLOPS = 2 * BATCH * GATES * (D_IN + 2 * STATE)


def tile_lngru2dcell_kernel(
    tc, x, s_prev0, s_prev1, Wi_words, Wi_scales, Ws_words, Ws_scales,
    lni_g, lni_b, lns_g, lns_b, lnh_g, lnh_b, out,
):
    nc = tc.nc
    with ExitStack() as ctx:
        keep = ctx.enter_context(tc.tile_pool(name="keep", bufs=1))
        stage = ctx.enter_context(tc.tile_pool(name="stage", bufs=2))
        blend = ctx.enter_context(tc.tile_pool(name="blend", bufs=3))
        stat = ctx.enter_context(tc.tile_pool(name="stat", bufs=4))
        psum_gain = ctx.enter_context(tc.psum_pool(name="psum_gain", bufs=1))
        psum_acc = ctx.enter_context(tc.psum_pool(name="psum_acc", bufs=2))
        psum_bias = ctx.enter_context(tc.psum_pool(name="psum_bias", bufs=2))
        ctx.enter_context(tc.manual_schedule())

        x_sb = keep.tile([P, BATCH_TILES, D_IN], BF16)
        p0_sb = keep.tile([P, BATCH_TILES, STATE], BF16)
        p1_sb = keep.tile([P, BATCH_TILES, STATE], BF16)
        wi_words = keep.tile([P, GATES], U32, align_bytes=64)
        ws_words = keep.tile([P, STATE_PASSES, GATES], U32, align_bytes=64)
        wi_plane = keep.tile([P, GATES], U8, align_bytes=64)
        ws_planes = keep.tile([P, GATES], U8, align_bytes=64)
        n_operands = BATCH_TILES * (1 + STATE_PASSES)
        act_codes = keep.tile([P, n_operands, P], U32, align_bytes=64)
        act_scales = keep.tile([P, n_operands, P], U8, align_bytes=64)
        rows = keep.tile([P, GATES], BF16)
        vec_rows = keep.tile([P, P], BF16)
        vec_cols = keep.tile([P, P], BF16)
        ident = keep.tile([P, P], F32)
        ident_bf = keep.tile([P, P], BF16)
        pick = keep.tile([P, 4, P], BF16)
        neg_half = keep.tile([P, 1], F32)
        zero_col = keep.tile([P, 1], F32)
        warm_col = keep.tile([P, 1], F32)
        squares = keep.tile([P, 2 * BANK], F32)
        ig_tiles = [keep.tile([P, GATES], F32, name="ig%d" % i) for i in range(3)]
        sg_tiles = [keep.tile([P, GATES], F32, name="sg%d" % i) for i in range(2)]

        nc.vector.memset(wi_plane[:].bitcast(I32), 0)
        nc.vector.memset(ws_planes[:].bitcast(I32), 0)
        nc.vector.memset(zero_col[:], 0.0)
        nc.vector.memset(neg_half[:], -0.5)
        nc.vector.memset(rows[:].bitcast(I32), 0)
        nc.vector.memset(vec_rows[:].bitcast(I32), 0)
        nc.vector.memset(pick[:], 0.0)
        PICK_LNS_G, PICK_BOTH_B, PICK_LNI_B, PICK_LNS_B = 0, 1, 2, 3
        nc.vector.memset(pick[ROW_LNS_G : ROW_LNS_G + 1, PICK_LNS_G, :], 1.0)
        nc.vector.memset(pick[ROW_LNI_B : ROW_LNI_B + 1, PICK_BOTH_B, :], 1.0)
        nc.vector.memset(pick[ROW_LNS_B : ROW_LNS_B + 1, PICK_BOTH_B, :], 1.0)
        nc.vector.memset(pick[ROW_LNI_B : ROW_LNI_B + 1, PICK_LNI_B, :], 1.0)
        nc.vector.memset(pick[ROW_LNS_B : ROW_LNS_B + 1, PICK_LNS_B, :], 1.0)
        make_identity(nc, ident[:])
        make_identity(nc, ident_bf[:])
        nc.scalar.activation(out=warm_col[:], in_=zero_col[:], func=ACT.Sigmoid)

        nc.sync.dma_start(out=x_sb[:], in_=x.rearrange("(m p) d -> p m d", p=P))
        nc.sync.dma_start(out=rows[ROW_LNS_G : ROW_LNS_G + 1, :], in_=lns_g.unsqueeze(0))
        nc.sync.dma_start(out=rows[ROW_LNI_B : ROW_LNI_B + 1, :], in_=lni_b.unsqueeze(0))
        nc.sync.dma_start(out=rows[ROW_LNS_B : ROW_LNS_B + 1, :], in_=lns_b.unsqueeze(0))
        for vector, col, length in ((lni_g, COL_LNI_G, GATES), (lnh_g, COL_LNH_G, STATE), (lnh_b, COL_LNH_B, STATE)):
            nc.sync.dma_start(
                out=vec_rows[col : col + length // P, :], in_=vector.rearrange("(c p) -> c p", p=P)
            )
        for quad in range(4):
            nc.sync.dma_start(
                out=wi_plane[32 * quad : 32 * quad + 4, :].bitcast(I32),
                in_=Wi_scales[0, 4 * quad : 4 * quad + 4, :].bitcast(I32),
            )
        wi_dram = Wi_words[0].rearrange("p n t -> p (n t)").bitcast(I32)
        for c in range(4):
            cols = slice(c * STATE, (c + 1) * STATE)
            nc.sync.dma_start(out=wi_words[:, cols].bitcast(I32), in_=wi_dram[:, cols])
        nc.sync.dma_start(out=p0_sb[:], in_=s_prev0.rearrange("(m p) d -> p m d", p=P))
        nc.sync.dma_start(out=p1_sb[:], in_=s_prev1.rearrange("(m p) d -> p m d", p=P))
        for quad in range(4):
            nc.sync.dma_start(
                out=ws_planes[32 * quad : 32 * quad + 16, :].bitcast(I32),
                in_=Ws_scales[:, 4 * quad : 4 * quad + 4, :].bitcast(I32),
            )
        ws_dram = Ws_words.rearrange("g p n t -> p g (n t)").bitcast(I32)
        for n in range(BANKS_PER_ROW):
            cols = slice(n * BANK, (n + 1) * BANK)
            nc.sync.dma_start(out=ws_words[:, :, cols].bitcast(I32), in_=ws_dram[:, :, cols])

        def quantise_round(first_operand, sources, scalar_helps):
            grouped = stage.tile([P, ROUND, P, PACK], BF16, align_bytes=64)
            grouped_words = grouped[:].rearrange("p c b t -> p (c b t)").bitcast(F32)
            for half in range(2):
                flipped = psum_acc.tile([P, 4, P], F32, tag="acc")
                for c in range(2):
                    for u in range(2):
                        nc.tensor.transpose(
                            flipped[:, 2 * c + u, :], sources[2 * half + c][:, u:WORDS:2], ident[:]
                        )
                dst = grouped_words[:, half * BANK : (half + 1) * BANK]
                dst = dst.rearrange("p (c b u) -> p c b u", c=2, u=2)
                src = flipped[:].rearrange("p (c u) b -> p c b u", u=2)
                if half == 1 and scalar_helps:
                    nc.scalar.copy(out=dst, in_=src)
                else:
                    nc.vector.tensor_copy(out=dst, in_=src)
            taken = slice(first_operand, first_operand + ROUND)
            nc.vector.quantize_mx(
                out=act_codes[:, taken, :].rearrange("p c b -> p (c b)").bitcast(FP8X4),
                scales=act_scales[:, taken, :].rearrange("p c b -> p (c b)"),
                in_=grouped[:].rearrange("p c b t -> p (c b t)"),
            )

        quantise_round(0, [x_sb[:, m, :].bitcast(F32) for m in range(BATCH_TILES)], True)

        lns_g_banks = []
        for c in range(4):
            gain = psum_gain.tile([P, STATE], BF16, name="lns_g_bank%d" % c)
            for h in range(2):
                nc.tensor.matmul(
                    out=gain[:, h * BANK : (h + 1) * BANK],
                    lhsT=pick[:, PICK_LNS_G, :],
                    rhs=rows[:, c * STATE + h * BANK : c * STATE + (h + 1) * BANK],
                    start=True,
                    stop=True,
                )
            lns_g_banks.append(gain)

        flipped_rows = psum_bias.tile([P, P], BF16, tag="bias")
        nc.tensor.transpose(flipped_rows[:], vec_rows[:], ident_bf[:])
        nc.vector.tensor_copy(out=vec_cols[:], in_=flipped_rows[:])

        def repeat(first_col):
            bank = psum_bias.tile([P, STATE], BF16, tag="bias")
            for j in range(STATE // P):
                nc.tensor.transpose(
                    bank[:, j * P : (j + 1) * P],
                    vec_cols[:, first_col + j : first_col + j + 1].to_broadcast([P, P]),
                    ident_bf[:],
                )
            return bank

        def quantise_states(m):
            p0_words = p0_sb[:, m, :].bitcast(F32)
            p1_words = p1_sb[:, m, :].bitcast(F32)
            quantise_round(
                BATCH_TILES + STATE_PASSES * m,
                [p0_words[:, 0:WORDS], p0_words[:, WORDS : 2 * WORDS],
                 p1_words[:, 0:WORDS], p1_words[:, WORDS : 2 * WORDS]],
                False,
            )

        def bank_cols(n):
            return slice(n * BANK, (n + 1) * BANK)

        def row_total(parts, width, factor):
            scaled = stat.tile([P, BANKS_PER_ROW], F32)
            total = stat.tile([P, 1], F32)
            nc.scalar.activation(
                out=scaled[:, 0:width], in_=parts[:], func=ACT.Copy, scale=factor, accum_out=total[:]
            )
            return total

        def rsqrt(variance):
            shifted = stat.tile([P, 1], F32)
            nc.gpsimd.tensor_scalar(
                out=shifted[:], in0=variance, scalar1=1.0, scalar2=EPS, op0=ALU.mult, op1=ALU.add
            )
            rstd = stat.tile([P, 1], F32)
            nc.gpsimd.tensor_tensor(out=rstd[:], in0=shifted[:], in1=neg_half[:], op=ALU.pow)
            return rstd

        n_matrices = 2 * BATCH_TILES
        sums_of = {}
        norm_of = {}

        def raw_tile(matrix):
            m = matrix // 2
            return sg_tiles[m % 2] if matrix % 2 else ig_tiles[m % 3]

        first_chunks = stat.tile([P, BANKS_PER_ROW, 6], F32)

        def first_statistics(n, values):
            nc.vector.bn_stats(out=first_chunks[:, n, :], in_=values)
            if n == BANKS_PER_ROW - 1:
                first_mean_var = stat.tile([P, 2], F32)
                nc.vector.bn_aggr(out=first_mean_var[:], in_=first_chunks[:].rearrange("p a b -> p (a b)"))
                first_neg_mean = stat.tile([P, 1], F32)
                nc.scalar.mul(out=first_neg_mean[:], in_=first_mean_var[:, 0:1], mul=-1.0)
                norm_of[0] = (first_neg_mean, rsqrt(first_mean_var[:, 1:2]))

        def sweep_step(matrix, n):
            m = matrix // 2
            if matrix % 2:
                first = BATCH_TILES + STATE_PASSES * m
                passes = [(first + g, ws_words[:, g, :], ws_planes[4 * g : P, :]) for g in range(STATE_PASSES)]
            else:
                passes = [(m, wi_words, wi_plane)]
            raw = raw_tile(matrix)
            cols = bank_cols(n)
            if n == 0:
                bank_sums = stat.tile([P, BANKS_PER_ROW], F32)
                bank_squares = stat.tile([P, BANKS_PER_ROW // 2], F32)
                neg_shift = stat.tile([P, 1], F32)
                sums_of[matrix] = (bank_sums, bank_squares, neg_shift)
            bank_sums, bank_squares, neg_shift = sums_of[matrix]
            acc = psum_acc.tile([P, BANK], F32, tag="acc")
            for j, (operand, words, plane) in enumerate(passes):
                nc.tensor.matmul_mx(
                    out=acc[:],
                    lhsT=act_codes[:, operand, :].bitcast(FP8X4),
                    lhsT_scale=act_scales[:, operand, :],
                    rhs=words[:, cols].bitcast(FP8X4),
                    rhs_scale=plane[:, cols],
                    start=(j == 0),
                    stop=(j == len(passes) - 1),
                )
            if matrix == 0:
                nc.scalar.copy(out=raw[:, cols], in_=acc[:])
                first_statistics(n, raw[:, cols])
                return
            nc.scalar.activation(out=raw[:, cols], in_=acc[:], func=ACT.Copy, accum_out=bank_sums[:, n : n + 1])
            if n == 0:
                nc.scalar.mul(out=neg_shift[:], in_=bank_sums[:, 0:1], mul=-1.0 / BANK)
            if n % 2 == 1:
                nc.scalar.activation(
                    out=squares[:], in_=raw[:, (n - 1) * BANK : (n + 1) * BANK], func=ACT.Square,
                    bias=neg_shift[:, 0:1], scale=1.0, accum_out=bank_squares[:, n // 2 : n // 2 + 1],
                )
            if n == BANKS_PER_ROW - 1:
                neg_mean = row_total(bank_sums, BANKS_PER_ROW, -1.0 / GATES)
                mean_square = row_total(bank_squares, BANKS_PER_ROW // 2, 1.0 / GATES)
                offset_square = stat.tile([P, 1], F32)
                nc.scalar.activation(
                    out=offset_square[:], in_=neg_mean[:], func=ACT.Square, bias=neg_shift[:, 0:1], scale=-1.0
                )
                variance = stat.tile([P, 1], F32)
                nc.gpsimd.tensor_tensor(out=variance[:], in0=mean_square[:], in1=offset_square[:], op=ALU.subtract)
                norm_of[matrix] = (neg_mean, rsqrt(variance[:]))

        def centre_and_gain(matrix, block, gain):
            raw = raw_tile(matrix)
            nc.vector.scalar_tensor_tensor(
                out=raw[:, block], in0=raw[:, block], scalar=norm_of[matrix][0][:, 0:1], in1=gain,
                op0=ALU.add, op1=ALU.mult,
            )

        def scale_and_bias(matrix, cols, picked):
            raw = raw_tile(matrix)
            bias = psum_bias.tile([P, BANK], F32, tag="bias")
            nc.tensor.matmul(out=bias[:], lhsT=pick[:, picked, :], rhs=rows[:, cols], start=True, stop=True)
            nc.vector.scalar_tensor_tensor(
                out=raw[:, cols], in0=raw[:, cols], scalar=norm_of[matrix][1][:, 0:1], in1=bias[:],
                op0=ALU.mult, op1=ALU.add,
            )

        def input_step(m, n):
            if n < 4:
                block = slice(n * STATE, (n + 1) * STATE)
                centre_and_gain(2 * m, block, repeat(COL_LNI_G + n * (STATE // P))[:])
            else:
                for bank in (2 * (n - 4), 2 * (n - 4) + 1):
                    in_cand = CAND_FIRST <= bank * BANK < CAND_FIRST + STATE
                    scale_and_bias(2 * m, bank_cols(bank), PICK_LNI_B if in_cand else PICK_BOTH_B)

        mix_of = {}
        last_norm_of = {}
        block_order = [RESET, CAND, LERP, INPUT]
        gain_bank_of_block = [0, 2, 3, 1]

        def state_step(m, t):
            ig = ig_tiles[m % 3]
            sg = sg_tiles[m % 2]
            p0 = p0_sb[:, m, :]
            p1 = p1_sb[:, m, :]
            rstd = norm_of[2 * m + 1][1]
            helper = nc.vector if m == BATCH_TILES - 1 else nc.gpsimd
            if t < 4:
                centre_and_gain(2 * m + 1, block_order[t], lns_g_banks[gain_bank_of_block[t]][:])
            if t == 4:
                for h in range(2):
                    scale_and_bias(2 * m + 1, bank_cols(CAND_FIRST // BANK + h), PICK_LNS_B)
                mix_of[m] = blend.tile([P, STATE], F32, name="mix")
                helper.tensor_tensor(out=mix_of[m][:], in0=p0, in1=p1, op=ALU.subtract)
            if t in (5, 6, 7):
                block = (RESET, LERP, INPUT)[t - 5]
                nc.vector.scalar_tensor_tensor(
                    out=sg[:, block], in0=sg[:, block], scalar=rstd[:, 0:1], in1=ig[:, block],
                    op0=ALU.mult, op1=ALU.add,
                )
            if t == 7:
                nc.scalar.activation(out=sg[:, RESET], in_=sg[:, RESET], func=ACT.Sigmoid, scale=-1.0)
            if t == 8:
                nc.scalar.activation(out=sg[:, LERP], in_=sg[:, LERP], func=ACT.Sigmoid)
            if t == 9:
                nc.scalar.activation(out=sg[:, INPUT], in_=sg[:, INPUT], func=ACT.Sigmoid)
            if t == 9:
                helper.tensor_tensor(out=sg[:, CAND], in0=sg[:, CAND], in1=sg[:, RESET], op=ALU.mult)
                helper.tensor_tensor(out=sg[:, CAND], in0=sg[:, CAND], in1=ig[:, CAND], op=ALU.add)
            if t == 12:
                nc.scalar.activation(out=sg[:, CAND], in_=sg[:, CAND], func=ACT.Tanh)
                mix = mix_of[m]
                helper.tensor_tensor(out=mix[:], in0=mix[:], in1=sg[:, LERP], op=ALU.mult)
                helper.tensor_tensor(out=mix[:], in0=mix[:], in1=p1, op=ALU.add)
                helper.tensor_tensor(out=mix[:], in0=mix[:], in1=sg[:, CAND], op=ALU.subtract)
                helper.tensor_tensor(out=mix[:], in0=mix[:], in1=sg[:, INPUT], op=ALU.mult)
                helper.tensor_tensor(out=mix[:], in0=mix[:], in1=sg[:, CAND], op=ALU.add)
            if t == 23:
                mix = mix_of[m]
                chunk_stats = stat.tile([P, 2, 6], F32)
                for h in range(2):
                    nc.vector.bn_stats(out=chunk_stats[:, h, :], in_=mix[:, bank_cols(h)])
                mean_var = stat.tile([P, 2], F32)
                nc.vector.bn_aggr(out=mean_var[:], in_=chunk_stats[:].rearrange("p a b -> p (a b)"))
                last_norm_of[m] = (mean_var, rsqrt(mean_var[:, 1:2]))
            if t == 30:
                mix = mix_of[m]
                nc.vector.scalar_tensor_tensor(
                    out=mix[:], in0=mix[:], scalar=last_norm_of[m][0][:, 0:1], in1=repeat(COL_LNH_G)[:],
                    op0=ALU.subtract, op1=ALU.mult,
                )
            if t == 31:
                mix = mix_of[m]
                nc.vector.scalar_tensor_tensor(
                    out=mix[:], in0=mix[:], scalar=last_norm_of[m][1][:, 0:1], in1=repeat(COL_LNH_B)[:],
                    op0=ALU.mult, op1=ALU.add,
                )
                nc.sync.dma_start(out=out[m * P : (m + 1) * P, :], in_=mix[:])

        sweep_order = [0, 2, 1, 4, 3, 6, 5, 7]
        state_steps = 32
        for k in range(n_matrices + state_steps // BANKS_PER_ROW):
            for n in range(BANKS_PER_ROW):
                if k < n_matrices:
                    sweep_step(sweep_order[k], n)
                for m in range(BATCH_TILES):
                    t = (k - sweep_order.index(2 * m + 1) - 1) * BANKS_PER_ROW + n
                    if 0 <= t < state_steps:
                        state_step(m, t)
                    if k == sweep_order.index(2 * m) + 1:
                        input_step(m, n)
            if k < BATCH_TILES:
                quantise_states(k)
